import numpy as np
import ml_dtypes

BF16 = ml_dtypes.bfloat16


def bf(x):
    return np.asarray(x, np.float32).astype(BF16)


def f32(x):
    return np.asarray(x, np.float32)


def f64(x):
    return np.asarray(x).astype(np.float64)


def striped(idx):
    return np.tile(idx.reshape(-1, 16).T, (8, 1))


C, C3, S, N, H, HD, T, NM = 512, 1536, 4096, 2048, 4, 128, 128, 4


def setup_inputs():
    return {
        "x": bf(np.random.standard_normal((C, N))),
        "qkv_w": bf(np.random.standard_normal((C, C3)) / np.sqrt(C)),
        "q_b": f32(0.1 * np.random.standard_normal((C, 1))),
        "v_b": f32(0.1 * np.random.standard_normal((C, 1))),
        "rel_bias": f32(0.5 * np.random.standard_normal((H, T, T))),
        "mask": f32(0.3 * np.random.standard_normal((NM, T, T))),
        "proj_w": bf(4.0 * np.random.standard_normal((C, C)) / np.sqrt(C)),
        "proj_b": f32(0.3 * np.random.standard_normal((C, 1))),
        "base": f32(np.random.standard_normal((C, S))),
        "offs": striped(np.random.permutation(S)[:N]),
    }


def reference(x, qkv_w, q_b, v_b, rel_bias, mask, proj_w, proj_b, base, offs):
    idx = offs[:16].T.reshape(-1)
    xx, w = f64(x), f64(qkv_w)
    q = (w[:, :C].T @ xx + f64(q_b)) / np.sqrt(HD)
    k = w[:, C:C3 - C].T @ xx
    v = w[:, C3 - C:].T @ xx + f64(v_b)
    q = q.reshape(H, HD, N // T, T)
    k = k.reshape(H, HD, N // T, T)
    v = v.reshape(H, HD, N // T, T)
    s = np.einsum("hdbn,hdbm->bhnm", q, k)
    s = s + f64(rel_bias)[None] + np.tile(f64(mask), (N // T // NM, 1, 1))[:, None]
    e = np.exp(s - s.max(axis=-1, keepdims=True))
    p = e / e.sum(axis=-1, keepdims=True)
    a = np.einsum("bhnm,hdbm->hdbn", p, v).reshape(C, N)
    out = f64(base).copy()
    out[:, idx] = f64(proj_w).T @ a + f64(proj_b)
    return out

@@ -1,0 +1,163 @@
+import math
+
+import concourse.mybir as mybir
+from concourse.masks import make_identity
+
+P = 128
+C = 512
+N = 2048
+S = 4096
+H = 4
+HD = 128
+T = 128
+NM = 4
+CB = C // P
+NW = N // T
+CHUNK = 512
+NCH = N // CHUNK
+WPC = CHUNK // T
+
+FLOPS = 2 * C * 3 * C * N + 2 * 2 * NW * H * T * T * HD + 2 * C * C * N
+
+BF16, F32, U16 = mybir.dt.bfloat16, mybir.dt.float32, mybir.dt.uint16
+ADD, MULT, MAX = mybir.AluOpType.add, mybir.AluOpType.mult, mybir.AluOpType.max
+EXP = mybir.ActivationFunctionType.Exp
+IDENTITY = mybir.ActivationFunctionType.Identity
+
+
+def tile_windowattention_b_kernel(
+    tc, x, qkv_w, q_b, v_b, rel_bias, mask, proj_w, proj_b, base, offs, out
+):
+    nc = tc.nc
+    inv_sqrt_hd = 1.0 / math.sqrt(HD)
+    with (
+        tc.tile_pool(name="held", bufs=1) as held,
+        tc.tile_pool(name="chunked", bufs=2) as chunked,
+        tc.tile_pool(name="work", bufs=3) as work,
+        tc.tile_pool(name="stats", bufs=4) as stats,
+        tc.psum_pool(name="acc", bufs=4) as acc,
+        tc.psum_pool(name="scores", bufs=2) as scores,
+        tc.psum_pool(name="flipped", bufs=1) as flipped,
+        tc.psum_pool(name="attended", bufs=1) as attended,
+    ):
+        offsets = held.tile([P, N // 16], U16, name="offsets")
+        nc.sync.dma_start(offsets[:], offs)
+
+        x_sb = [[held.tile([P, CHUNK], BF16, name=f"x{cb}_{t}") for t in range(NCH)] for cb in range(CB)]
+        for t in range(NCH):
+            for cb in range(CB):
+                nc.sync.dma_start(x_sb[cb][t][:], x[cb * P : (cb + 1) * P, t * CHUNK : (t + 1) * CHUNK])
+        w_q = [held.tile([P, C], BF16, name=f"w_q{cb}") for cb in range(CB)]
+        w_k = [held.tile([P, C], BF16, name=f"w_k{cb}") for cb in range(CB)]
+        w_v = [held.tile([P, C], BF16, name=f"w_v{cb}") for cb in range(CB)]
+        for part, w_part in ((1, w_k), (0, w_q), (2, w_v)):
+            for cb in range(CB):
+                nc.scalar.dma_start(w_part[cb][:], qkv_w[cb * P : (cb + 1) * P, part * C : (part + 1) * C])
+        w_p = [held.tile([P, C], BF16, name=f"w_p{cb}") for cb in range(CB)]
+        for cb in range(CB):
+            nc.scalar.dma_start(w_p[cb][:], proj_w[cb * P : (cb + 1) * P, :])
+
+        q_b_sb = held.tile([P, CB], F32, name="q_b_sb")
+        proj_b_sb = held.tile([P, CB], F32, name="proj_b_sb")
+        with nc.allow_non_contiguous_dma(reason="512 biases, one to a partition and column"):
+            nc.gpsimd.dma_start(q_b_sb[:], q_b.rearrange("(k p) one -> p (k one)", p=P))
+            nc.gpsimd.dma_start(proj_b_sb[:], proj_b.rearrange("(k p) one -> p (k one)", p=P))
+        v_b_rows = held.tile([P, C], F32, name="v_b_rows")
+        nc.gpsimd.dma_start(v_b_rows[:], v_b.rearrange("c one -> (c one)").partition_broadcast(P))
+        rel_sb = held.tile([P, H, T], F32, name="rel_sb")
+        nc.gpsimd.dma_start(rel_sb[:], rel_bias.rearrange("h n m -> n h m"))
+        mask_sb = held.tile([P, NM, T], F32, name="mask_sb")
+        nc.gpsimd.dma_start(mask_sb[:], mask.rearrange("i n m -> n i m"))
+
+        window = [held.tile([P, S], F32, name=f"window{ob}") for ob in range(CB)]
+        for ob in range(CB):
+            nc.sync.dma_start(window[ob][:], base[ob * P : (ob + 1) * P, :])
+
+        ident = held.tile([P, P], BF16, name="ident")
+        make_identity(nc, ident[:])
+        q_b_scaled = held.tile([P, CB], F32, name="q_b_scaled")
+        nc.gpsimd.tensor_scalar_mul(q_b_scaled[:], q_b_sb[:], inv_sqrt_hd)
+        score_bias = [held.tile([P, H, T], F32, name=f"score_bias{i}") for i in range(NM)]
+        for i in range(NM):
+            nc.gpsimd.tensor_tensor(
+                score_bias[i][:], rel_sb[:], mask_sb[:, i, :].unsqueeze(1).to_broadcast([P, H, T]), ADD
+            )
+
+        proj_b_rows = [held.tile([P, N], F32, name=f"proj_b_rows{ob}") for ob in range(CB)]
+        for ob in range(CB):
+            nc.gpsimd.tensor_copy(proj_b_rows[ob][:], proj_b_sb[:, ob : ob + 1].to_broadcast([P, N]))
+
+        v_sb = [held.tile([P, C], BF16, name=f"v{b}") for b in range(NW)]
+        a_sb = [held.tile([P, H, CHUNK], BF16, name=f"a{t}") for t in range(NCH)]
+
+        for t in range(NCH):
+            k_sb = chunked.tile([P, H, CHUNK], BF16, name="k_sb")
+            q_sb = chunked.tile([P, H, CHUNK], BF16, name="q_sb")
+            for h in range(H):
+                k_ps = acc.tile([P, CHUNK], F32, name="acc_ps")
+                for cb in range(CB):
+                    nc.tensor.matmul(
+                        k_ps[:], w_k[cb][:, h * HD : (h + 1) * HD], x_sb[cb][t][:], start=(cb == 0), stop=(cb == CB - 1)
+                    )
+                nc.vector.tensor_copy(k_sb[:, h, :], k_ps[:])
+            for h in range(H):
+                q_ps = acc.tile([P, CHUNK], F32, name="acc_ps")
+                for cb in range(CB):
+                    nc.tensor.matmul(
+                        q_ps[:], w_q[cb][:, h * HD : (h + 1) * HD], x_sb[cb][t][:], start=(cb == 0), stop=(cb == CB - 1)
+                    )
+                nc.scalar.activation(
+                    q_sb[:, h, :], q_ps[:], IDENTITY, bias=q_b_scaled[:, h : h + 1], scale=inv_sqrt_hd
+                )
+            for w in range(WPC):
+                v_ps = acc.tile([P, C], F32, name="acc_ps")
+                for cb in range(CB):
+                    nc.tensor.matmul(
+                        v_ps[:], x_sb[cb][t][:, w * T : (w + 1) * T], w_v[cb][:], start=(cb == 0), stop=(cb == CB - 1)
+                    )
+                nc.vector.tensor_tensor(v_sb[t * WPC + w][:], v_ps[:], v_b_rows[:], ADD)
+
+            for w in range(WPC):
+                b = t * WPC + w
+                tokens = slice(w * T, (w + 1) * T)
+                s_ps = scores.tile([P, H, T], F32, name="s_ps")
+                for h in range(H):
+                    nc.tensor.matmul(s_ps[:, h, :], q_sb[:, h, tokens], k_sb[:, h, tokens], start=True, stop=True)
+                s_sb = work.tile([P, H, T], F32, name="s_sb")
+                nc.vector.tensor_tensor(s_sb[:], s_ps[:], score_bias[b % NM][:], ADD)
+                neg_max = stats.tile([P, H], F32, name="neg_max")
+                nc.vector.tensor_reduce(neg_max[:], s_sb[:], axis=mybir.AxisListType.X, op=MAX, negate=True)
+                e_sb = work.tile([P, H, T], F32, name="e_sb")
+                e_sum = stats.tile([P, H], F32, name="e_sum")
+                for h in range(H):
+                    nc.scalar.activation(
+                        e_sb[:, h, :], s_sb[:, h, :], EXP, bias=neg_max[:, h : h + 1], scale=1.0,
+                        accum_out=e_sum[:, h : h + 1],
+                    )
+                r_sum = stats.tile([P, H], F32, name="r_sum")
+                nc.vector.reciprocal(r_sum[:], e_sum[:])
+                p_sb = work.tile([P, H, T], BF16, name="p_sb")
+                nc.gpsimd.tensor_tensor(p_sb[:], e_sb[:], r_sum[:].unsqueeze(2).to_broadcast([P, H, T]), MULT)
+                pT_ps = flipped.tile([P, H, T], BF16, name="pT_ps")
+                for h in range(H):
+                    nc.tensor.transpose(pT_ps[:, h, :], p_sb[:, h, :], ident[:])
+                pT_sb = work.tile([P, H, T], BF16, name="pT_sb")
+                nc.vector.tensor_copy(pT_sb[:], pT_ps[:])
+                a_ps = attended.tile([P, H, T], F32, name="a_ps")
+                for h in range(H):
+                    nc.tensor.matmul(a_ps[:, h, :], v_sb[b][:, h * HD : (h + 1) * HD], pT_sb[:, h, :], start=True, stop=True)
+                nc.scalar.copy(a_sb[t][:, :, tokens], a_ps[:])
+
+        for ob in range(CB):
+            y_sb = chunked.tile([P, N], F32, name="y_sb")
+            for t in range(NCH):
+                y_ps = acc.tile([P, CHUNK], F32, name="acc_ps")
+                for h in range(H):
+                    nc.tensor.matmul(
+                        y_ps[:], w_p[h][:, ob * P : (ob + 1) * P], a_sb[t][:, h, :], start=(h == 0), stop=(h == H - 1)
+                    )
+                nc.scalar.copy(y_sb[:, t * CHUNK : (t + 1) * CHUNK], y_ps[:])
+            nc.vector.tensor_tensor(
+                window[ob][:].indirect(offsets[:]), y_sb[:], proj_b_rows[ob][:], ADD
+            )
+            nc.sync.dma_start(out[ob * P : (ob + 1) * P, :], window[ob][:])

@@ -34,6 +34,7 @@ def tile_windowattention_b_kernel(
         tc.tile_pool(name="held", bufs=1) as held,
         tc.tile_pool(name="chunked", bufs=2) as chunked,
         tc.tile_pool(name="work", bufs=3) as work,
+        tc.tile_pool(name="probs", bufs=2 * WPC) as probs,
         tc.tile_pool(name="stats", bufs=4) as stats,
         tc.psum_pool(name="acc", bufs=4) as acc,
         tc.psum_pool(name="scores", bufs=2) as scores,
@@ -83,70 +84,83 @@ def tile_windowattention_b_kernel(
                 score_bias[i][:], rel_sb[:], mask_sb[:, i, :].unsqueeze(1).to_broadcast([P, H, T]), ADD
             )
 
+        v_sb = [held.tile([P, C], BF16, name=f"v{b}") for b in range(NW)]
+        a_sb = [held.tile([P, H, CHUNK], BF16, name=f"a{t}") for t in range(NCH)]
+        p_sb = {}
+
+        for t in range(NCH + 1):
+            if t < NCH:
+                k_sb = chunked.tile([P, H, CHUNK], BF16, name="k_sb")
+                q_sb = chunked.tile([P, H, CHUNK], BF16, name="q_sb")
+                for h in range(H):
+                    k_ps = acc.tile([P, CHUNK], F32, name="acc_ps")
+                    for cb in range(CB):
+                        nc.tensor.matmul(
+                            k_ps[:], w_k[cb][:, h * HD : (h + 1) * HD], x_sb[cb][t][:],
+                            start=(cb == 0), stop=(cb == CB - 1),
+                        )
+                    nc.vector.tensor_copy(k_sb[:, h, :], k_ps[:])
+                for h in range(H):
+                    q_ps = acc.tile([P, CHUNK], F32, name="acc_ps")
+                    for cb in range(CB):
+                        nc.tensor.matmul(
+                            q_ps[:], w_q[cb][:, h * HD : (h + 1) * HD], x_sb[cb][t][:],
+                            start=(cb == 0), stop=(cb == CB - 1),
+                        )
+                    nc.scalar.activation(
+                        q_sb[:, h, :], q_ps[:], IDENTITY, bias=q_b_scaled[:, h : h + 1], scale=inv_sqrt_hd
+                    )
+
+                for w in range(WPC):
+                    b = t * WPC + w
+                    tokens = slice(w * T, (w + 1) * T)
+                    s_ps = scores.tile([P, H, T], F32, name="s_ps")
+                    for h in range(H):
+                        nc.tensor.matmul(s_ps[:, h, :], q_sb[:, h, tokens], k_sb[:, h, tokens], start=True, stop=True)
+                    s_sb = work.tile([P, H, T], F32, name="s_sb")
+                    nc.vector.tensor_tensor(s_sb[:], s_ps[:], score_bias[b % NM][:], ADD)
+                    neg_max = stats.tile([P, H], F32, name="neg_max")
+                    nc.vector.tensor_reduce(neg_max[:], s_sb[:], axis=mybir.AxisListType.X, op=MAX, negate=True)
+                    e_sb = work.tile([P, H, T], F32, name="e_sb")
+                    e_sum = stats.tile([P, H], F32, name="e_sum")
+                    for h in range(H):
+                        nc.scalar.activation(
+                            e_sb[:, h, :], s_sb[:, h, :], EXP, bias=neg_max[:, h : h + 1], scale=1.0,
+                            accum_out=e_sum[:, h : h + 1],
+                        )
+                    r_sum = stats.tile([P, H], F32, name="r_sum")
+                    nc.vector.reciprocal(r_sum[:], e_sum[:])
+                    p_sb[b] = probs.tile([P, H, T], BF16, name="p_sb")
+                    nc.gpsimd.tensor_tensor(p_sb[b][:], e_sb[:], r_sum[:].unsqueeze(2).to_broadcast([P, H, T]), MULT)
+
+            if t > 0:
+                for w in range(WPC):
+                    b = (t - 1) * WPC + w
+                    v_ps = acc.tile([P, C], F32, name="acc_ps")
+                    for cb in range(CB):
+                        nc.tensor.matmul(
+                            v_ps[:], x_sb[cb][t - 1][:, w * T : (w + 1) * T], w_v[cb][:],
+                            start=(cb == 0), stop=(cb == CB - 1),
+                        )
+                    nc.vector.tensor_tensor(v_sb[b][:], v_ps[:], v_b_rows[:], ADD)
+
+                for w in range(WPC):
+                    b = (t - 1) * WPC + w
+                    pT_ps = flipped.tile([P, H, T], BF16, name="pT_ps")
+                    for h in range(H):
+                        nc.tensor.transpose(pT_ps[:, h, :], p_sb[b][:, h, :], ident[:])
+                    pT_sb = work.tile([P, H, T], BF16, name="pT_sb")
+                    nc.vector.tensor_copy(pT_sb[:], pT_ps[:])
+                    a_ps = attended.tile([P, H, T], F32, name="a_ps")
+                    for h in range(H):
+                        nc.tensor.matmul(
+                            a_ps[:, h, :], v_sb[b][:, h * HD : (h + 1) * HD], pT_sb[:, h, :], start=True, stop=True
+                        )
+                    nc.scalar.copy(a_sb[t - 1][:, :, w * T : (w + 1) * T], a_ps[:])
+
         proj_b_rows = [held.tile([P, N], F32, name=f"proj_b_rows{ob}") for ob in range(CB)]
         for ob in range(CB):
             nc.gpsimd.tensor_copy(proj_b_rows[ob][:], proj_b_sb[:, ob : ob + 1].to_broadcast([P, N]))
-
-        v_sb = [held.tile([P, C], BF16, name=f"v{b}") for b in range(NW)]
-        a_sb = [held.tile([P, H, CHUNK], BF16, name=f"a{t}") for t in range(NCH)]
-
-        for t in range(NCH):
-            k_sb = chunked.tile([P, H, CHUNK], BF16, name="k_sb")
-            q_sb = chunked.tile([P, H, CHUNK], BF16, name="q_sb")
-            for h in range(H):
-                k_ps = acc.tile([P, CHUNK], F32, name="acc_ps")
-                for cb in range(CB):
-                    nc.tensor.matmul(
-                        k_ps[:], w_k[cb][:, h * HD : (h + 1) * HD], x_sb[cb][t][:], start=(cb == 0), stop=(cb == CB - 1)
-                    )
-                nc.vector.tensor_copy(k_sb[:, h, :], k_ps[:])
-            for h in range(H):
-                q_ps = acc.tile([P, CHUNK], F32, name="acc_ps")
-                for cb in range(CB):
-                    nc.tensor.matmul(
-                        q_ps[:], w_q[cb][:, h * HD : (h + 1) * HD], x_sb[cb][t][:], start=(cb == 0), stop=(cb == CB - 1)
-                    )
-                nc.scalar.activation(
-                    q_sb[:, h, :], q_ps[:], IDENTITY, bias=q_b_scaled[:, h : h + 1], scale=inv_sqrt_hd
-                )
-            for w in range(WPC):
-                v_ps = acc.tile([P, C], F32, name="acc_ps")
-                for cb in range(CB):
-                    nc.tensor.matmul(
-                        v_ps[:], x_sb[cb][t][:, w * T : (w + 1) * T], w_v[cb][:], start=(cb == 0), stop=(cb == CB - 1)
-                    )
-                nc.vector.tensor_tensor(v_sb[t * WPC + w][:], v_ps[:], v_b_rows[:], ADD)
-
-            for w in range(WPC):
-                b = t * WPC + w
-                tokens = slice(w * T, (w + 1) * T)
-                s_ps = scores.tile([P, H, T], F32, name="s_ps")
-                for h in range(H):
-                    nc.tensor.matmul(s_ps[:, h, :], q_sb[:, h, tokens], k_sb[:, h, tokens], start=True, stop=True)
-                s_sb = work.tile([P, H, T], F32, name="s_sb")
-                nc.vector.tensor_tensor(s_sb[:], s_ps[:], score_bias[b % NM][:], ADD)
-                neg_max = stats.tile([P, H], F32, name="neg_max")
-                nc.vector.tensor_reduce(neg_max[:], s_sb[:], axis=mybir.AxisListType.X, op=MAX, negate=True)
-                e_sb = work.tile([P, H, T], F32, name="e_sb")
-                e_sum = stats.tile([P, H], F32, name="e_sum")
-                for h in range(H):
-                    nc.scalar.activation(
-                        e_sb[:, h, :], s_sb[:, h, :], EXP, bias=neg_max[:, h : h + 1], scale=1.0,
-                        accum_out=e_sum[:, h : h + 1],
-                    )
-                r_sum = stats.tile([P, H], F32, name="r_sum")
-                nc.vector.reciprocal(r_sum[:], e_sum[:])
-                p_sb = work.tile([P, H, T], BF16, name="p_sb")
-                nc.gpsimd.tensor_tensor(p_sb[:], e_sb[:], r_sum[:].unsqueeze(2).to_broadcast([P, H, T]), MULT)
-                pT_ps = flipped.tile([P, H, T], BF16, name="pT_ps")
-                for h in range(H):
-                    nc.tensor.transpose(pT_ps[:, h, :], p_sb[:, h, :], ident[:])
-                pT_sb = work.tile([P, H, T], BF16, name="pT_sb")
-                nc.vector.tensor_copy(pT_sb[:], pT_ps[:])
-                a_ps = attended.tile([P, H, T], F32, name="a_ps")
-                for h in range(H):
-                    nc.tensor.matmul(a_ps[:, h, :], v_sb[b][:, h * HD : (h + 1) * HD], pT_sb[:, h, :], start=True, stop=True)
-                nc.scalar.copy(a_sb[t][:, :, tokens], a_ps[:])
 
         for ob in range(CB):
             y_sb = chunked.tile([P, N], F32, name="y_sb")
@@ -157,7 +171,5 @@ def tile_windowattention_b_kernel(
                         y_ps[:], w_p[h][:, ob * P : (ob + 1) * P], a_sb[t][:, h, :], start=(h == 0), stop=(h == H - 1)
                     )
                 nc.scalar.copy(y_sb[:, t * CHUNK : (t + 1) * CHUNK], y_ps[:])
-            nc.vector.tensor_tensor(
-                window[ob][:].indirect(offsets[:]), y_sb[:], proj_b_rows[ob][:], ADD
-            )
+            nc.vector.tensor_tensor(window[ob][:].indirect(offsets[:]), y_sb[:], proj_b_rows[ob][:], ADD)
             nc.sync.dma_start(out[ob * P : (ob + 1) * P, :], window[ob][:])

@@ -48,6 +48,12 @@ def tile_windowattention_b_kernel(
         for t in range(NCH):
             for cb in range(CB):
                 nc.sync.dma_start(x_sb[cb][t][:], x[cb * P : (cb + 1) * P, t * CHUNK : (t + 1) * CHUNK])
+            if t == 0:
+                q_b_sb = held.tile([P, CB], F32, name="q_b_sb")
+                proj_b_sb = held.tile([P, CB], F32, name="proj_b_sb")
+                with nc.allow_non_contiguous_dma(reason="512 biases, one to a partition and column"):
+                    nc.sync.dma_start(q_b_sb[:], q_b.rearrange("(k p) one -> p (k one)", p=P))
+                    nc.sync.dma_start(proj_b_sb[:], proj_b.rearrange("(k p) one -> p (k one)", p=P))
         w_q = [held.tile([P, C], BF16, name=f"w_q{cb}") for cb in range(CB)]
         w_k = [held.tile([P, C], BF16, name=f"w_k{cb}") for cb in range(CB)]
         w_v = [held.tile([P, C], BF16, name=f"w_v{cb}") for cb in range(CB)]
@@ -58,11 +64,6 @@ def tile_windowattention_b_kernel(
         for cb in range(CB):
             nc.scalar.dma_start(w_p[cb][:], proj_w[cb * P : (cb + 1) * P, :])
 
-        q_b_sb = held.tile([P, CB], F32, name="q_b_sb")
-        proj_b_sb = held.tile([P, CB], F32, name="proj_b_sb")
-        with nc.allow_non_contiguous_dma(reason="512 biases, one to a partition and column"):
-            nc.gpsimd.dma_start(q_b_sb[:], q_b.rearrange("(k p) one -> p (k one)", p=P))
-            nc.gpsimd.dma_start(proj_b_sb[:], proj_b.rearrange("(k p) one -> p (k one)", p=P))
         v_b_rows = held.tile([P, C], F32, name="v_b_rows")
         nc.gpsimd.dma_start(v_b_rows[:], v_b.rearrange("c one -> (c one)").partition_broadcast(P))
         rel_sb = held.tile([P, H, T], F32, name="rel_sb")
@@ -144,8 +145,6 @@ def tile_windowattention_b_kernel(
                         )
                     nc.vector.tensor_tensor(v_sb[b][:], v_ps[:], v_b_rows[:], ADD)
 
-                for w in range(WPC):
-                    b = (t - 1) * WPC + w
                     pT_ps = flipped.tile([P, H, T], BF16, name="pT_ps")
                     for h in range(H):
                         nc.tensor.transpose(pT_ps[:, h, :], p_sb[b][:, h, :], ident[:])

@@ -147,7 +147,7 @@ def tile_windowattention_b_kernel(
 
                     pT_ps = flipped.tile([P, H, T], BF16, name="pT_ps")
                     for h in range(H):
-                        nc.tensor.transpose(pT_ps[:, h, :], p_sb[b][:, h, :], ident[:])
+                        nc.tensor.matmul(pT_ps[:, h, :], p_sb[b][:, h, :], ident[:], start=True, stop=True)
                     pT_sb = work.tile([P, H, T], BF16, name="pT_sb")
                     nc.vector.tensor_copy(pT_sb[:], pT_ps[:])
                     a_ps = attended.tile([P, H, T], F32, name="a_ps")

@@ -44,32 +44,33 @@ def tile_windowattention_b_kernel(
         offsets = held.tile([P, N // 16], U16, name="offsets")
         nc.sync.dma_start(offsets[:], offs)
 
-        x_sb = [[held.tile([P, CHUNK], BF16, name=f"x{cb}_{t}") for t in range(NCH)] for cb in range(CB)]
-        for t in range(NCH):
-            for cb in range(CB):
-                nc.sync.dma_start(x_sb[cb][t][:], x[cb * P : (cb + 1) * P, t * CHUNK : (t + 1) * CHUNK])
-            if t == 0:
-                q_b_sb = held.tile([P, CB], F32, name="q_b_sb")
-                proj_b_sb = held.tile([P, CB], F32, name="proj_b_sb")
-                with nc.allow_non_contiguous_dma(reason="512 biases, one to a partition and column"):
-                    nc.sync.dma_start(q_b_sb[:], q_b.rearrange("(k p) one -> p (k one)", p=P))
-                    nc.sync.dma_start(proj_b_sb[:], proj_b.rearrange("(k p) one -> p (k one)", p=P))
-        w_q = [held.tile([P, C], BF16, name=f"w_q{cb}") for cb in range(CB)]
-        w_k = [held.tile([P, C], BF16, name=f"w_k{cb}") for cb in range(CB)]
-        w_v = [held.tile([P, C], BF16, name=f"w_v{cb}") for cb in range(CB)]
-        for part, w_part in ((1, w_k), (0, w_q), (2, w_v)):
-            for cb in range(CB):
-                nc.scalar.dma_start(w_part[cb][:], qkv_w[cb * P : (cb + 1) * P, part * C : (part + 1) * C])
-        w_p = [held.tile([P, C], BF16, name=f"w_p{cb}") for cb in range(CB)]
+        x_blocks = x.rearrange("(cb p) n -> p cb n", p=P)
+        qkv_blocks = qkv_w.rearrange("(cb p) o -> p cb o", p=P)
+        x_sb = [held.tile([P, CB, CHUNK], BF16, name=f"x{t}") for t in range(NCH)]
+        w_q = held.tile([P, CB, C], BF16, name="w_q")
+        w_k = held.tile([P, CB, C], BF16, name="w_k")
+        w_v = held.tile([P, CB, C], BF16, name="w_v")
+        w_p = held.tile([P, CB, C], BF16, name="w_p")
+        q_b_sb = held.tile([P, CB], F32, name="q_b_sb")
+        proj_b_sb = held.tile([P, CB], F32, name="proj_b_sb")
         for cb in range(CB):
-            nc.scalar.dma_start(w_p[cb][:], proj_w[cb * P : (cb + 1) * P, :])
+            nc.sync.dma_start(x_sb[0][:, cb, :], x_blocks[:, cb, 0:CHUNK])
+            nc.scalar.dma_start(w_k[:, cb, :], qkv_blocks[:, cb, C : 2 * C])
+        with nc.allow_non_contiguous_dma(reason="512 biases, one to a partition and column"):
+            nc.sync.dma_start(q_b_sb[:], q_b.rearrange("(k p) one -> p (k one)", p=P))
+            nc.sync.dma_start(proj_b_sb[:], proj_b.rearrange("(k p) one -> p (k one)", p=P))
+        for t in range(1, NCH):
+            nc.sync.dma_start(x_sb[t][:], x_blocks[:, :, t * CHUNK : (t + 1) * CHUNK])
+        nc.scalar.dma_start(w_q[:], qkv_blocks[:, :, 0:C])
+        nc.scalar.dma_start(w_v[:], qkv_blocks[:, :, 2 * C : 3 * C])
+        nc.scalar.dma_start(w_p[:], proj_w.rearrange("(cb p) o -> p cb o", p=P))
 
-        v_b_rows = held.tile([P, C], F32, name="v_b_rows")
-        nc.gpsimd.dma_start(v_b_rows[:], v_b.rearrange("c one -> (c one)").partition_broadcast(P))
         rel_sb = held.tile([P, H, T], F32, name="rel_sb")
         nc.gpsimd.dma_start(rel_sb[:], rel_bias.rearrange("h n m -> n h m"))
         mask_sb = held.tile([P, NM, T], F32, name="mask_sb")
         nc.gpsimd.dma_start(mask_sb[:], mask.rearrange("i n m -> n i m"))
+        v_b_rows = held.tile([P, C], F32, name="v_b_rows")
+        nc.gpsimd.dma_start(v_b_rows[:], v_b.rearrange("c one -> (c one)").partition_broadcast(P))
 
         window = [held.tile([P, S], F32, name=f"window{ob}") for ob in range(CB)]
         for ob in range(CB):
@@ -97,7 +98,7 @@ def tile_windowattention_b_kernel(
                     k_ps = acc.tile([P, CHUNK], F32, name="acc_ps")
                     for cb in range(CB):
                         nc.tensor.matmul(
-                            k_ps[:], w_k[cb][:, h * HD : (h + 1) * HD], x_sb[cb][t][:],
+                            k_ps[:], w_k[:, cb, h * HD : (h + 1) * HD], x_sb[t][:, cb, :],
                             start=(cb == 0), stop=(cb == CB - 1),
                         )
                     nc.vector.tensor_copy(k_sb[:, h, :], k_ps[:])
@@ -105,7 +106,7 @@ def tile_windowattention_b_kernel(
                     q_ps = acc.tile([P, CHUNK], F32, name="acc_ps")
                     for cb in range(CB):
                         nc.tensor.matmul(
-                            q_ps[:], w_q[cb][:, h * HD : (h + 1) * HD], x_sb[cb][t][:],
+                            q_ps[:], w_q[:, cb, h * HD : (h + 1) * HD], x_sb[t][:, cb, :],
                             start=(cb == 0), stop=(cb == CB - 1),
                         )
                     nc.scalar.activation(
@@ -140,14 +141,14 @@ def tile_windowattention_b_kernel(
                     v_ps = acc.tile([P, C], F32, name="acc_ps")
                     for cb in range(CB):
                         nc.tensor.matmul(
-                            v_ps[:], x_sb[cb][t - 1][:, w * T : (w + 1) * T], w_v[cb][:],
+                            v_ps[:], x_sb[t - 1][:, cb, w * T : (w + 1) * T], w_v[:, cb, :],
                             start=(cb == 0), stop=(cb == CB - 1),
                         )
                     nc.vector.tensor_tensor(v_sb[b][:], v_ps[:], v_b_rows[:], ADD)
 
                     pT_ps = flipped.tile([P, H, T], BF16, name="pT_ps")
                     for h in range(H):
-                        nc.tensor.matmul(pT_ps[:, h, :], p_sb[b][:, h, :], ident[:], start=True, stop=True)
+                        nc.tensor.transpose(pT_ps[:, h, :], p_sb[b][:, h, :], ident[:])
                     pT_sb = work.tile([P, H, T], BF16, name="pT_sb")
                     nc.vector.tensor_copy(pT_sb[:], pT_ps[:])
                     a_ps = attended.tile([P, H, T], F32, name="a_ps")
@@ -167,7 +168,7 @@ def tile_windowattention_b_kernel(
                 y_ps = acc.tile([P, CHUNK], F32, name="acc_ps")
                 for h in range(H):
                     nc.tensor.matmul(
-                        y_ps[:], w_p[h][:, ob * P : (ob + 1) * P], a_sb[t][:, h, :], start=(h == 0), stop=(h == H - 1)
+                        y_ps[:], w_p[:, h, ob * P : (ob + 1) * P], a_sb[t][:, h, :], start=(h == 0), stop=(h == H - 1)
                     )
                 nc.scalar.copy(y_sb[:, t * CHUNK : (t + 1) * CHUNK], y_ps[:])
             nc.vector.tensor_tensor(window[ob][:].indirect(offsets[:]), y_sb[:], proj_b_rows[ob][:], ADD)

@@ -16,6 +16,7 @@ NW = N // T
 CHUNK = 512
 NCH = N // CHUNK
 WPC = CHUNK // T
+LAG = 4
 
 FLOPS = 2 * C * 3 * C * N + 2 * 2 * NW * H * T * T * HD + 2 * C * C * N
 
@@ -33,11 +34,11 @@ def tile_windowattention_b_kernel(
     with (
         tc.tile_pool(name="held", bufs=1) as held,
         tc.tile_pool(name="chunked", bufs=2) as chunked,
-        tc.tile_pool(name="work", bufs=3) as work,
-        tc.tile_pool(name="probs", bufs=2 * WPC) as probs,
+        tc.tile_pool(name="ring", bufs=3) as ring,
+        tc.tile_pool(name="probs", bufs=LAG + 2) as probs,
         tc.tile_pool(name="stats", bufs=4) as stats,
         tc.psum_pool(name="acc", bufs=4) as acc,
-        tc.psum_pool(name="scores", bufs=2) as scores,
+        tc.psum_pool(name="scored", bufs=2) as scored,
         tc.psum_pool(name="flipped", bufs=1) as flipped,
         tc.psum_pool(name="attended", bufs=1) as attended,
     ):
@@ -86,90 +87,137 @@ def tile_windowattention_b_kernel(
                 score_bias[i][:], rel_sb[:], mask_sb[:, i, :].unsqueeze(1).to_broadcast([P, H, T]), ADD
             )
 
-        v_sb = [held.tile([P, C], BF16, name=f"v{b}") for b in range(NW)]
+        k_sb, q_sb = {}, {}
+        v_sb = {}
+        s_sb, neg_max, e_sb, e_sum = {}, {}, {}, {}
+        p_sb, pT_sb = {}, {}
         a_sb = [held.tile([P, H, CHUNK], BF16, name=f"a{t}") for t in range(NCH)]
-        p_sb = {}
+        y_sb = {}
 
-        for t in range(NCH + 1):
-            if t < NCH:
-                k_sb = chunked.tile([P, H, CHUNK], BF16, name="k_sb")
-                q_sb = chunked.tile([P, H, CHUNK], BF16, name="q_sb")
-                for h in range(H):
-                    k_ps = acc.tile([P, CHUNK], F32, name="acc_ps")
-                    for cb in range(CB):
-                        nc.tensor.matmul(
-                            k_ps[:], w_k[:, cb, h * HD : (h + 1) * HD], x_sb[t][:, cb, :],
-                            start=(cb == 0), stop=(cb == CB - 1),
-                        )
-                    nc.vector.tensor_copy(k_sb[:, h, :], k_ps[:])
-                for h in range(H):
-                    q_ps = acc.tile([P, CHUNK], F32, name="acc_ps")
-                    for cb in range(CB):
-                        nc.tensor.matmul(
-                            q_ps[:], w_q[:, cb, h * HD : (h + 1) * HD], x_sb[t][:, cb, :],
-                            start=(cb == 0), stop=(cb == CB - 1),
-                        )
-                    nc.scalar.activation(
-                        q_sb[:, h, :], q_ps[:], IDENTITY, bias=q_b_scaled[:, h : h + 1], scale=inv_sqrt_hd
-                    )
+        def project_k(t, h):
+            if h == 0:
+                k_sb[t] = chunked.tile([P, H, CHUNK], BF16, name="k_sb")
+            k_ps = acc.tile([P, CHUNK], F32, name="acc_ps")
+            for cb in range(CB):
+                nc.tensor.matmul(
+                    k_ps[:], w_k[:, cb, h * HD : (h + 1) * HD], x_sb[t][:, cb, :], start=(cb == 0), stop=(cb == CB - 1)
+                )
+            nc.vector.tensor_copy(k_sb[t][:, h, :], k_ps[:])
 
-                for w in range(WPC):
-                    b = t * WPC + w
-                    tokens = slice(w * T, (w + 1) * T)
-                    s_ps = scores.tile([P, H, T], F32, name="s_ps")
-                    for h in range(H):
-                        nc.tensor.matmul(s_ps[:, h, :], q_sb[:, h, tokens], k_sb[:, h, tokens], start=True, stop=True)
-                    s_sb = work.tile([P, H, T], F32, name="s_sb")
-                    nc.vector.tensor_tensor(s_sb[:], s_ps[:], score_bias[b % NM][:], ADD)
-                    neg_max = stats.tile([P, H], F32, name="neg_max")
-                    nc.vector.tensor_reduce(neg_max[:], s_sb[:], axis=mybir.AxisListType.X, op=MAX, negate=True)
-                    e_sb = work.tile([P, H, T], F32, name="e_sb")
-                    e_sum = stats.tile([P, H], F32, name="e_sum")
-                    for h in range(H):
-                        nc.scalar.activation(
-                            e_sb[:, h, :], s_sb[:, h, :], EXP, bias=neg_max[:, h : h + 1], scale=1.0,
-                            accum_out=e_sum[:, h : h + 1],
-                        )
-                    r_sum = stats.tile([P, H], F32, name="r_sum")
-                    nc.vector.reciprocal(r_sum[:], e_sum[:])
-                    p_sb[b] = probs.tile([P, H, T], BF16, name="p_sb")
-                    nc.gpsimd.tensor_tensor(p_sb[b][:], e_sb[:], r_sum[:].unsqueeze(2).to_broadcast([P, H, T]), MULT)
+        def project_q(t, h):
+            if h == 0:
+                q_sb[t] = chunked.tile([P, H, CHUNK], BF16, name="q_sb")
+            q_ps = acc.tile([P, CHUNK], F32, name="acc_ps")
+            for cb in range(CB):
+                nc.tensor.matmul(
+                    q_ps[:], w_q[:, cb, h * HD : (h + 1) * HD], x_sb[t][:, cb, :], start=(cb == 0), stop=(cb == CB - 1)
+                )
+            nc.scalar.activation(
+                q_sb[t][:, h, :], q_ps[:], IDENTITY, bias=q_b_scaled[:, h : h + 1], scale=inv_sqrt_hd
+            )
 
-            if t > 0:
-                for w in range(WPC):
-                    b = (t - 1) * WPC + w
-                    v_ps = acc.tile([P, C], F32, name="acc_ps")
-                    for cb in range(CB):
-                        nc.tensor.matmul(
-                            v_ps[:], x_sb[t - 1][:, cb, w * T : (w + 1) * T], w_v[:, cb, :],
-                            start=(cb == 0), stop=(cb == CB - 1),
-                        )
-                    nc.vector.tensor_tensor(v_sb[b][:], v_ps[:], v_b_rows[:], ADD)
+        def project_v(b):
+            t, w = divmod(b, WPC)
+            v_ps = acc.tile([P, C], F32, name="acc_ps")
+            for cb in range(CB):
+                nc.tensor.matmul(
+                    v_ps[:], x_sb[t][:, cb, w * T : (w + 1) * T], w_v[:, cb, :], start=(cb == 0), stop=(cb == CB - 1)
+                )
+            v_sb[b] = ring.tile([P, C], BF16, name="v_sb")
+            nc.vector.tensor_tensor(v_sb[b][:], v_ps[:], v_b_rows[:], ADD)
 
-                    pT_ps = flipped.tile([P, H, T], BF16, name="pT_ps")
-                    for h in range(H):
-                        nc.tensor.transpose(pT_ps[:, h, :], p_sb[b][:, h, :], ident[:])
-                    pT_sb = work.tile([P, H, T], BF16, name="pT_sb")
-                    nc.vector.tensor_copy(pT_sb[:], pT_ps[:])
-                    a_ps = attended.tile([P, H, T], F32, name="a_ps")
-                    for h in range(H):
-                        nc.tensor.matmul(
-                            a_ps[:, h, :], v_sb[b][:, h * HD : (h + 1) * HD], pT_sb[:, h, :], start=True, stop=True
-                        )
-                    nc.scalar.copy(a_sb[t - 1][:, :, w * T : (w + 1) * T], a_ps[:])
+        def scores(b):
+            t, w = divmod(b, WPC)
+            tokens = slice(w * T, (w + 1) * T)
+            s_ps = scored.tile([P, H, T], F32, name="s_ps")
+            for h in range(H):
+                nc.tensor.matmul(s_ps[:, h, :], q_sb[t][:, h, tokens], k_sb[t][:, h, tokens], start=True, stop=True)
+            s_sb[b] = ring.tile([P, H, T], F32, name="s_sb")
+            nc.vector.tensor_tensor(s_sb[b][:], s_ps[:], score_bias[b % NM][:], ADD)
+            neg_max[b] = stats.tile([P, H], F32, name="neg_max")
+            nc.vector.tensor_reduce(neg_max[b][:], s_sb[b][:], axis=mybir.AxisListType.X, op=MAX, negate=True)
+
+        def exponentials(b):
+            e_sb[b] = ring.tile([P, H, T], F32, name="e_sb")
+            e_sum[b] = stats.tile([P, H], F32, name="e_sum")
+            for h in range(H):
+                nc.scalar.activation(
+                    e_sb[b][:, h, :], s_sb[b][:, h, :], EXP, bias=neg_max[b][:, h : h + 1], scale=1.0,
+                    accum_out=e_sum[b][:, h : h + 1],
+                )
+
+        def normalise(b):
+            r_sum = stats.tile([P, H], F32, name="r_sum")
+            nc.vector.reciprocal(r_sum[:], e_sum[b][:])
+            p_sb[b] = probs.tile([P, H, T], BF16, name="p_sb")
+            nc.gpsimd.tensor_tensor(p_sb[b][:], e_sb[b][:], r_sum[:].unsqueeze(2).to_broadcast([P, H, T]), MULT)
+
+        def flip(b):
+            pT_ps = flipped.tile([P, H, T], BF16, name="pT_ps")
+            for h in range(H):
+                nc.tensor.transpose(pT_ps[:, h, :], p_sb[b][:, h, :], ident[:])
+            pT_sb[b] = ring.tile([P, H, T], BF16, name="pT_sb")
+            nc.vector.tensor_copy(pT_sb[b][:], pT_ps[:])
+
+        def attend(b):
+            t, w = divmod(b, WPC)
+            a_ps = attended.tile([P, H, T], F32, name="a_ps")
+            for h in range(H):
+                nc.tensor.matmul(
+                    a_ps[:, h, :], v_sb[b][:, h * HD : (h + 1) * HD], pT_sb[b][:, h, :], start=True, stop=True
+                )
+            nc.scalar.copy(a_sb[t][:, :, w * T : (w + 1) * T], a_ps[:])
+
+        def project_y(ob, t):
+            if t == 0:
+                y_sb[ob] = chunked.tile([P, N], F32, name="y_sb")
+            y_ps = acc.tile([P, CHUNK], F32, name="acc_ps")
+            for h in range(H):
+                nc.tensor.matmul(
+                    y_ps[:], w_p[:, h, ob * P : (ob + 1) * P], a_sb[t][:, h, :], start=(h == 0), stop=(h == H - 1)
+                )
+            nc.scalar.copy(y_sb[ob][:, t * CHUNK : (t + 1) * CHUNK], y_ps[:])
+
+        k_sb[0] = chunked.tile([P, H, CHUNK], BF16, name="k_sb")
+        k_ps = [acc.tile([P, CHUNK], F32, name="acc_ps") for h in range(H)]
+        for cb in range(CB):
+            for h in range(H):
+                nc.tensor.matmul(
+                    k_ps[h][:], w_k[:, cb, h * HD : (h + 1) * HD], x_sb[0][:, cb, :], start=(cb == 0), stop=(cb == CB - 1)
+                )
+        for h in range(H):
+            nc.vector.tensor_copy(k_sb[0][:, h, :], k_ps[h][:])
+        for h in range(H):
+            project_q(0, h)
+        for i in range(NW + LAG + 1):
+            t, w = divmod(i, WPC)
+            done = i - LAG
+            if 0 <= done < NW:
+                flip(done)
+            if 1 <= i <= NW:
+                normalise(i - 1)
+            if 0 <= done + 1 < NW:
+                project_v(done + 1)
+            if done >= WPC and done % WPC == 0:
+                project_y(0, done // WPC - 1)
+            if t + 1 < NCH:
+                project_k(t + 1, w)
+            if i < NW:
+                scores(i)
+            if 0 <= done < NW:
+                attend(done)
+            if t + 1 < NCH:
+                project_q(t + 1, w)
+            if i < NW:
+                exponentials(i)
 
         proj_b_rows = [held.tile([P, N], F32, name=f"proj_b_rows{ob}") for ob in range(CB)]
         for ob in range(CB):
             nc.gpsimd.tensor_copy(proj_b_rows[ob][:], proj_b_sb[:, ob : ob + 1].to_broadcast([P, N]))
 
         for ob in range(CB):
-            y_sb = chunked.tile([P, N], F32, name="y_sb")
-            for t in range(NCH):
-                y_ps = acc.tile([P, CHUNK], F32, name="acc_ps")
-                for h in range(H):
-                    nc.tensor.matmul(
-                        y_ps[:], w_p[:, h, ob * P : (ob + 1) * P], a_sb[t][:, h, :], start=(h == 0), stop=(h == H - 1)
-                    )
-                nc.scalar.copy(y_sb[:, t * CHUNK : (t + 1) * CHUNK], y_ps[:])
-            nc.vector.tensor_tensor(window[ob][:].indirect(offsets[:]), y_sb[:], proj_b_rows[ob][:], ADD)
+            if ob > 0:
+                for t in range(NCH):
+                    project_y(ob, t)
+            nc.vector.tensor_tensor(window[ob][:].indirect(offsets[:]), y_sb[ob][:], proj_b_rows[ob][:], ADD)
             nc.sync.dma_start(out[ob * P : (ob + 1) * P, :], window[ob][:])

@@ -42,11 +42,9 @@ def tile_windowattention_b_kernel(
         tc.psum_pool(name="flipped", bufs=1) as flipped,
         tc.psum_pool(name="attended", bufs=1) as attended,
     ):
-        offsets = held.tile([P, N // 16], U16, name="offsets")
-        nc.sync.dma_start(offsets[:], offs)
-
         x_blocks = x.rearrange("(cb p) n -> p cb n", p=P)
         qkv_blocks = qkv_w.rearrange("(cb p) o -> p cb o", p=P)
+        offsets = held.tile([P, N // 16], U16, name="offsets")
         x_sb = [held.tile([P, CB, CHUNK], BF16, name=f"x{t}") for t in range(NCH)]
         w_q = held.tile([P, CB, C], BF16, name="w_q")
         w_k = held.tile([P, CB, C], BF16, name="w_k")
@@ -54,26 +52,29 @@ def tile_windowattention_b_kernel(
         w_p = held.tile([P, CB, C], BF16, name="w_p")
         q_b_sb = held.tile([P, CB], F32, name="q_b_sb")
         proj_b_sb = held.tile([P, CB], F32, name="proj_b_sb")
+        rel_sb = held.tile([P, H, T], F32, name="rel_sb")
+        mask_sb = held.tile([P, NM, T], F32, name="mask_sb")
+        v_b_rows = held.tile([P, C], F32, name="v_b_rows")
+        window = [held.tile([P, S], F32, name=f"window{ob}") for ob in range(CB)]
+
         for cb in range(CB):
             nc.sync.dma_start(x_sb[0][:, cb, :], x_blocks[:, cb, 0:CHUNK])
-            nc.scalar.dma_start(w_k[:, cb, :], qkv_blocks[:, cb, C : 2 * C])
+            nc.sync.dma_start(w_k[:, cb, :], qkv_blocks[:, cb, C : 2 * C])
+            if cb == 0:
+                with nc.allow_non_contiguous_dma(reason="512 biases, one to a partition and column"):
+                    nc.sync.dma_start(proj_b_sb[:], proj_b.rearrange("(k p) one -> p (k one)", p=P))
+        nc.sync.dma_start(w_q[:], qkv_blocks[:, :, 0:C])
         with nc.allow_non_contiguous_dma(reason="512 biases, one to a partition and column"):
             nc.sync.dma_start(q_b_sb[:], q_b.rearrange("(k p) one -> p (k one)", p=P))
-            nc.sync.dma_start(proj_b_sb[:], proj_b.rearrange("(k p) one -> p (k one)", p=P))
-        for t in range(1, NCH):
+        nc.sync.dma_start(rel_sb[:], rel_bias.rearrange("h n m -> n h m"))
+        nc.sync.dma_start(mask_sb[:], mask.rearrange("i n m -> n i m"))
+        nc.sync.dma_start(x_sb[1][:], x_blocks[:, :, CHUNK : 2 * CHUNK])
+        nc.sync.dma_start(w_v[:], qkv_blocks[:, :, 2 * C : 3 * C])
+        nc.sync.dma_start(v_b_rows[:], v_b.rearrange("c one -> (c one)").partition_broadcast(P))
+        for t in range(2, NCH):
             nc.sync.dma_start(x_sb[t][:], x_blocks[:, :, t * CHUNK : (t + 1) * CHUNK])
-        nc.scalar.dma_start(w_q[:], qkv_blocks[:, :, 0:C])
-        nc.scalar.dma_start(w_v[:], qkv_blocks[:, :, 2 * C : 3 * C])
-        nc.scalar.dma_start(w_p[:], proj_w.rearrange("(cb p) o -> p cb o", p=P))
-
-        rel_sb = held.tile([P, H, T], F32, name="rel_sb")
-        nc.gpsimd.dma_start(rel_sb[:], rel_bias.rearrange("h n m -> n h m"))
-        mask_sb = held.tile([P, NM, T], F32, name="mask_sb")
-        nc.gpsimd.dma_start(mask_sb[:], mask.rearrange("i n m -> n i m"))
-        v_b_rows = held.tile([P, C], F32, name="v_b_rows")
-        nc.gpsimd.dma_start(v_b_rows[:], v_b.rearrange("c one -> (c one)").partition_broadcast(P))
-
-        window = [held.tile([P, S], F32, name=f"window{ob}") for ob in range(CB)]
+        nc.sync.dma_start(w_p[:], proj_w.rearrange("(cb p) o -> p cb o", p=P))
+        nc.sync.dma_start(offsets[:], offs)
         for ob in range(CB):
             nc.sync.dma_start(window[ob][:], base[ob * P : (ob + 1) * P, :])
 
@@ -87,12 +88,16 @@ def tile_windowattention_b_kernel(
                 score_bias[i][:], rel_sb[:], mask_sb[:, i, :].unsqueeze(1).to_broadcast([P, H, T]), ADD
             )
 
+        proj_b_rows = [held.tile([P, N], F32, name=f"proj_b_rows{ob}") for ob in range(CB)]
+        for ob in range(CB):
+            nc.vector.tensor_copy(proj_b_rows[ob][:], proj_b_sb[:, ob : ob + 1].to_broadcast([P, N]))
+
         k_sb, q_sb = {}, {}
         v_sb = {}
         s_sb, neg_max, e_sb, e_sum = {}, {}, {}, {}
         p_sb, pT_sb = {}, {}
         a_sb = [held.tile([P, H, CHUNK], BF16, name=f"a{t}") for t in range(NCH)]
-        y_sb = {}
+        y_sb = [held.tile([P, N], F32, name=f"y{ob}") for ob in range(CB)]
 
         def project_k(t, h):
             if h == 0:
@@ -169,8 +174,6 @@ def tile_windowattention_b_kernel(
             nc.scalar.copy(a_sb[t][:, :, w * T : (w + 1) * T], a_ps[:])
 
         def project_y(ob, t):
-            if t == 0:
-                y_sb[ob] = chunked.tile([P, N], F32, name="y_sb")
             y_ps = acc.tile([P, CHUNK], F32, name="acc_ps")
             for h in range(H):
                 nc.tensor.matmul(
@@ -178,30 +181,23 @@ def tile_windowattention_b_kernel(
                 )
             nc.scalar.copy(y_sb[ob][:, t * CHUNK : (t + 1) * CHUNK], y_ps[:])
 
-        k_sb[0] = chunked.tile([P, H, CHUNK], BF16, name="k_sb")
-        k_ps = [acc.tile([P, CHUNK], F32, name="acc_ps") for h in range(H)]
-        for cb in range(CB):
-            for h in range(H):
-                nc.tensor.matmul(
-                    k_ps[h][:], w_k[:, cb, h * HD : (h + 1) * HD], x_sb[0][:, cb, :], start=(cb == 0), stop=(cb == CB - 1)
-                )
         for h in range(H):
-            nc.vector.tensor_copy(k_sb[0][:, h, :], k_ps[h][:])
+            project_k(0, h)
         for h in range(H):
             project_q(0, h)
-        for i in range(NW + LAG + 1):
+        for i in range(NW + LAG):
             t, w = divmod(i, WPC)
             done = i - LAG
-            if 0 <= done < NW:
-                flip(done)
-            if 1 <= i <= NW:
-                normalise(i - 1)
+            if 0 <= done + 1 < NW:
+                flip(done + 1)
+            if 0 <= done + 2 < NW:
+                normalise(done + 2)
             if 0 <= done + 1 < NW:
                 project_v(done + 1)
-            if done >= WPC and done % WPC == 0:
-                project_y(0, done // WPC - 1)
             if t + 1 < NCH:
                 project_k(t + 1, w)
+            elif w % 2 == 0 and (i - (NW - WPC)) // 2 < NCH - 1:
+                project_y(0, (i - (NW - WPC)) // 2)
             if i < NW:
                 scores(i)
             if 0 <= done < NW:
@@ -210,10 +206,7 @@ def tile_windowattention_b_kernel(
                 project_q(t + 1, w)
             if i < NW:
                 exponentials(i)
-
-        proj_b_rows = [held.tile([P, N], F32, name=f"proj_b_rows{ob}") for ob in range(CB)]
-        for ob in range(CB):
-            nc.gpsimd.tensor_copy(proj_b_rows[ob][:], proj_b_sb[:, ob : ob + 1].to_broadcast([P, N]))
+        project_y(0, NCH - 1)
 
         for ob in range(CB):
             if ob > 0:

@@ -92,6 +92,7 @@ def tile_windowattention_b_kernel(
         for ob in range(CB):
             nc.vector.tensor_copy(proj_b_rows[ob][:], proj_b_sb[:, ob : ob + 1].to_broadcast([P, N]))
 
+        k_ps, q_ps, v_ps, y_ps, s_ps, pT_ps, a_ps = {}, {}, {}, {}, {}, {}, {}
         k_sb, q_sb = {}, {}
         v_sb = {}
         s_sb, neg_max, e_sb, e_sum = {}, {}, {}, {}
@@ -99,50 +100,86 @@ def tile_windowattention_b_kernel(
         a_sb = [held.tile([P, H, CHUNK], BF16, name=f"a{t}") for t in range(NCH)]
         y_sb = [held.tile([P, N], F32, name=f"y{ob}") for ob in range(CB)]
 
-        def project_k(t, h):
-            if h == 0:
-                k_sb[t] = chunked.tile([P, H, CHUNK], BF16, name="k_sb")
-            k_ps = acc.tile([P, CHUNK], F32, name="acc_ps")
-            for cb in range(CB):
-                nc.tensor.matmul(
-                    k_ps[:], w_k[:, cb, h * HD : (h + 1) * HD], x_sb[t][:, cb, :], start=(cb == 0), stop=(cb == CB - 1)
-                )
-            nc.vector.tensor_copy(k_sb[t][:, h, :], k_ps[:])
-
-        def project_q(t, h):
-            if h == 0:
-                q_sb[t] = chunked.tile([P, H, CHUNK], BF16, name="q_sb")
-            q_ps = acc.tile([P, CHUNK], F32, name="acc_ps")
-            for cb in range(CB):
-                nc.tensor.matmul(
-                    q_ps[:], w_q[:, cb, h * HD : (h + 1) * HD], x_sb[t][:, cb, :], start=(cb == 0), stop=(cb == CB - 1)
-                )
-            nc.scalar.activation(
-                q_sb[t][:, h, :], q_ps[:], IDENTITY, bias=q_b_scaled[:, h : h + 1], scale=inv_sqrt_hd
+        def k_matmul(t, h, cb):
+            if t >= NCH:
+                return
+            if cb == 0:
+                k_ps[t, h] = acc.tile([P, CHUNK], F32, name="acc_ps")
+            nc.tensor.matmul(
+                k_ps[t, h][:], w_k[:, cb, h * HD : (h + 1) * HD], x_sb[t][:, cb, :], start=(cb == 0), stop=(cb == CB - 1)
             )
 
-        def project_v(b):
-            t, w = divmod(b, WPC)
-            v_ps = acc.tile([P, C], F32, name="acc_ps")
-            for cb in range(CB):
-                nc.tensor.matmul(
-                    v_ps[:], x_sb[t][:, cb, w * T : (w + 1) * T], w_v[:, cb, :], start=(cb == 0), stop=(cb == CB - 1)
-                )
-            v_sb[b] = ring.tile([P, C], BF16, name="v_sb")
-            nc.vector.tensor_tensor(v_sb[b][:], v_ps[:], v_b_rows[:], ADD)
+        def k_out(t, h):
+            if t >= NCH:
+                return
+            if h == 0:
+                k_sb[t] = chunked.tile([P, H, CHUNK], BF16, name="k_sb")
+            nc.vector.tensor_copy(k_sb[t][:, h, :], k_ps[t, h][:])
 
-        def scores(b):
+        def q_matmul(t, h, cb):
+            if t >= NCH:
+                return
+            if cb == 0:
+                q_ps[t, h] = acc.tile([P, CHUNK], F32, name="acc_ps")
+            nc.tensor.matmul(
+                q_ps[t, h][:], w_q[:, cb, h * HD : (h + 1) * HD], x_sb[t][:, cb, :], start=(cb == 0), stop=(cb == CB - 1)
+            )
+
+        def q_out(t, h):
+            if t >= NCH:
+                return
+            if h == 0:
+                q_sb[t] = chunked.tile([P, H, CHUNK], BF16, name="q_sb")
+            nc.scalar.activation(
+                q_sb[t][:, h, :], q_ps[t, h][:], IDENTITY, bias=q_b_scaled[:, h : h + 1], scale=inv_sqrt_hd
+            )
+
+        def v_matmul(b, cb):
+            if not 0 <= b < NW:
+                return
+            t, w = divmod(b, WPC)
+            if cb == 0:
+                v_ps[b] = acc.tile([P, C], F32, name="acc_ps")
+            nc.tensor.matmul(
+                v_ps[b][:], x_sb[t][:, cb, w * T : (w + 1) * T], w_v[:, cb, :], start=(cb == 0), stop=(cb == CB - 1)
+            )
+
+        def v_out(b):
+            if not 0 <= b < NW:
+                return
+            v_sb[b] = ring.tile([P, C], BF16, name="v_sb")
+            nc.vector.tensor_tensor(v_sb[b][:], v_ps[b][:], v_b_rows[:], ADD)
+
+        def y_matmul(ob, t, h):
+            if h == 0:
+                y_ps[ob, t] = acc.tile([P, CHUNK], F32, name="acc_ps")
+            nc.tensor.matmul(
+                y_ps[ob, t][:], w_p[:, h, ob * P : (ob + 1) * P], a_sb[t][:, h, :], start=(h == 0), stop=(h == H - 1)
+            )
+
+        def y_out(ob, t):
+            nc.scalar.copy(y_sb[ob][:, t * CHUNK : (t + 1) * CHUNK], y_ps[ob, t][:])
+
+        def score_matmul(b, h):
+            if not 0 <= b < NW:
+                return
             t, w = divmod(b, WPC)
             tokens = slice(w * T, (w + 1) * T)
-            s_ps = scored.tile([P, H, T], F32, name="s_ps")
-            for h in range(H):
-                nc.tensor.matmul(s_ps[:, h, :], q_sb[t][:, h, tokens], k_sb[t][:, h, tokens], start=True, stop=True)
+            if h == 0:
+                s_ps[b] = scored.tile([P, H, T], F32, name="s_ps")
+            nc.tensor.matmul(s_ps[b][:, h, :], q_sb[t][:, h, tokens], k_sb[t][:, h, tokens], start=True, stop=True)
+
+        def score_out(b):
+            if not 0 <= b < NW:
+                return
             s_sb[b] = ring.tile([P, H, T], F32, name="s_sb")
-            nc.vector.tensor_tensor(s_sb[b][:], s_ps[:], score_bias[b % NM][:], ADD)
+            nc.vector.tensor_tensor(s_sb[b][:], s_ps[b][:], score_bias[b % NM][:], ADD)
             neg_max[b] = stats.tile([P, H], F32, name="neg_max")
             nc.vector.tensor_reduce(neg_max[b][:], s_sb[b][:], axis=mybir.AxisListType.X, op=MAX, negate=True)
 
         def exponentials(b):
+            if not 0 <= b < NW:
+                return
             e_sb[b] = ring.tile([P, H, T], F32, name="e_sb")
             e_sum[b] = stats.tile([P, H], F32, name="e_sum")
             for h in range(H):
@@ -152,65 +189,84 @@ def tile_windowattention_b_kernel(
                 )
 
         def normalise(b):
+            if not 0 <= b < NW:
+                return
             r_sum = stats.tile([P, H], F32, name="r_sum")
             nc.vector.reciprocal(r_sum[:], e_sum[b][:])
             p_sb[b] = probs.tile([P, H, T], BF16, name="p_sb")
             nc.gpsimd.tensor_tensor(p_sb[b][:], e_sb[b][:], r_sum[:].unsqueeze(2).to_broadcast([P, H, T]), MULT)
 
-        def flip(b):
-            pT_ps = flipped.tile([P, H, T], BF16, name="pT_ps")
-            for h in range(H):
-                nc.tensor.transpose(pT_ps[:, h, :], p_sb[b][:, h, :], ident[:])
+        def flip_matmul(b, h):
+            if not 0 <= b < NW:
+                return
+            if h == 0:
+                pT_ps[b] = flipped.tile([P, H, T], BF16, name="pT_ps")
+            nc.tensor.transpose(pT_ps[b][:, h, :], p_sb[b][:, h, :], ident[:])
+
+        def flip_out(b):
+            if not 0 <= b < NW:
+                return
             pT_sb[b] = ring.tile([P, H, T], BF16, name="pT_sb")
-            nc.vector.tensor_copy(pT_sb[b][:], pT_ps[:])
+            nc.vector.tensor_copy(pT_sb[b][:], pT_ps[b][:])
 
-        def attend(b):
+        def attend_matmul(b, h):
+            if not 0 <= b < NW:
+                return
+            if h == 0:
+                a_ps[b] = attended.tile([P, H, T], F32, name="a_ps")
+            nc.tensor.matmul(
+                a_ps[b][:, h, :], v_sb[b][:, h * HD : (h + 1) * HD], pT_sb[b][:, h, :], start=True, stop=True
+            )
+
+        def attend_out(b):
+            if not 0 <= b < NW:
+                return
             t, w = divmod(b, WPC)
-            a_ps = attended.tile([P, H, T], F32, name="a_ps")
-            for h in range(H):
-                nc.tensor.matmul(
-                    a_ps[:, h, :], v_sb[b][:, h * HD : (h + 1) * HD], pT_sb[b][:, h, :], start=True, stop=True
-                )
-            nc.scalar.copy(a_sb[t][:, :, w * T : (w + 1) * T], a_ps[:])
-
-        def project_y(ob, t):
-            y_ps = acc.tile([P, CHUNK], F32, name="acc_ps")
-            for h in range(H):
-                nc.tensor.matmul(
-                    y_ps[:], w_p[:, h, ob * P : (ob + 1) * P], a_sb[t][:, h, :], start=(h == 0), stop=(h == H - 1)
-                )
-            nc.scalar.copy(y_sb[ob][:, t * CHUNK : (t + 1) * CHUNK], y_ps[:])
+            nc.scalar.copy(a_sb[t][:, :, w * T : (w + 1) * T], a_ps[b][:])
 
         for h in range(H):
-            project_k(0, h)
+            for cb in range(CB):
+                k_matmul(0, h, cb)
+            k_out(0, h)
         for h in range(H):
-            project_q(0, h)
+            for cb in range(CB):
+                q_matmul(0, h, cb)
+            q_out(0, h)
         for i in range(NW + LAG):
             t, w = divmod(i, WPC)
             done = i - LAG
-            if 0 <= done + 1 < NW:
-                flip(done + 1)
-            if 0 <= done + 2 < NW:
-                normalise(done + 2)
-            if 0 <= done + 1 < NW:
-                project_v(done + 1)
-            if t + 1 < NCH:
-                project_k(t + 1, w)
-            elif w % 2 == 0 and (i - (NW - WPC)) // 2 < NCH - 1:
-                project_y(0, (i - (NW - WPC)) // 2)
-            if i < NW:
-                scores(i)
-            if 0 <= done < NW:
-                attend(done)
-            if t + 1 < NCH:
-                project_q(t + 1, w)
-            if i < NW:
-                exponentials(i)
-        project_y(0, NCH - 1)
+            normalise(done + 2)
+            for j in range(4):
+                v_matmul(done + 1, j)
+                flip_matmul(done + 1, j)
+            flip_out(done + 1)
+            v_out(done + 1)
+            spare = (i - (NW - WPC)) // 2
+            fill_y = i >= NW - WPC and w % 2 == 0 and spare < NCH - 1
+            for j in range(4):
+                k_matmul(t + 1, w, j)
+                if fill_y:
+                    y_matmul(0, spare, j)
+                score_matmul(i, j)
+            k_out(t + 1, w)
+            if fill_y:
+                y_out(0, spare)
+            score_out(i)
+            for j in range(4):
+                q_matmul(t + 1, w, j)
+                attend_matmul(done, j)
+            attend_out(done)
+            q_out(t + 1, w)
+            exponentials(i)
+        for h in range(H):
+            y_matmul(0, NCH - 1, h)
+        y_out(0, NCH - 1)
 
         for ob in range(CB):
             if ob > 0:
                 for t in range(NCH):
-                    project_y(ob, t)
+                    for h in range(H):
+                        y_matmul(ob, t, h)
+                    y_out(ob, t)
             nc.vector.tensor_tensor(window[ob][:].indirect(offsets[:]), y_sb[ob][:], proj_b_rows[ob][:], ADD)
             nc.sync.dma_start(out[ob * P : (ob + 1) * P, :], window[ob][:])

@@ -150,15 +150,17 @@ def tile_windowattention_b_kernel(
             v_sb[b] = ring.tile([P, C], BF16, name="v_sb")
             nc.vector.tensor_tensor(v_sb[b][:], v_ps[b][:], v_b_rows[:], ADD)
 
-        def y_matmul(ob, t, h):
+        def y_matmul(ob, t, h, w0=0, w1=WPC):
             if h == 0:
-                y_ps[ob, t] = acc.tile([P, CHUNK], F32, name="acc_ps")
+                y_ps[ob, t, w0] = acc.tile([P, CHUNK], F32, name="acc_ps")
+            tokens = slice(w0 * T, w1 * T)
             nc.tensor.matmul(
-                y_ps[ob, t][:], w_p[:, h, ob * P : (ob + 1) * P], a_sb[t][:, h, :], start=(h == 0), stop=(h == H - 1)
+                y_ps[ob, t, w0][:, tokens], w_p[:, h, ob * P : (ob + 1) * P], a_sb[t][:, h, tokens],
+                start=(h == 0), stop=(h == H - 1),
             )
 
-        def y_out(ob, t):
-            nc.scalar.copy(y_sb[ob][:, t * CHUNK : (t + 1) * CHUNK], y_ps[ob, t][:])
+        def y_out(ob, t, w0=0, w1=WPC, copy=nc.scalar.copy):
+            copy(y_sb[ob][:, t * CHUNK + w0 * T : t * CHUNK + w1 * T], y_ps[ob, t, w0][:, w0 * T : w1 * T])
 
         def score_matmul(b, h):
             if not 0 <= b < NW:
@@ -232,7 +234,7 @@ def tile_windowattention_b_kernel(
             for cb in range(CB):
                 q_matmul(0, h, cb)
             q_out(0, h)
-        for i in range(NW + LAG):
+        for i in range(NW + LAG - 2):
             t, w = divmod(i, WPC)
             done = i - LAG
             normalise(done + 2)
@@ -242,7 +244,7 @@ def tile_windowattention_b_kernel(
             flip_out(done + 1)
             v_out(done + 1)
             spare = (i - (NW - WPC)) // 2
-            fill_y = i >= NW - WPC and w % 2 == 0 and spare < NCH - 1
+            fill_y = NW - WPC <= i < NW and w % 2 == 0
             for j in range(4):
                 k_matmul(t + 1, w, j)
                 if fill_y:
@@ -258,9 +260,28 @@ def tile_windowattention_b_kernel(
             attend_out(done)
             q_out(t + 1, w)
             exponentials(i)
+        last = NW - 1
         for h in range(H):
-            y_matmul(0, NCH - 1, h)
-        y_out(0, NCH - 1)
+            flip_matmul(last, h)
+        flip_out(last)
+        for cb in range(CB):
+            v_matmul(last, cb)
+        v_out(last)
+        for h in range(H):
+            attend_matmul(last - 1, h)
+        attend_out(last - 1)
+        for h in range(H):
+            y_matmul(0, NCH - 2, h)
+        y_out(0, NCH - 2)
+        for h in range(H):
+            attend_matmul(last, h)
+        attend_out(last)
+        for h in range(H):
+            y_matmul(0, NCH - 1, h, 0, WPC - 1)
+        y_out(0, NCH - 1, 0, WPC - 1, copy=nc.vector.tensor_copy)
+        for h in range(H):
+            y_matmul(0, NCH - 1, h, WPC - 1, WPC)
+        y_out(0, NCH - 1, WPC - 1, WPC)
 
         for ob in range(CB):
             if ob > 0:

@@ -59,7 +59,7 @@ def tile_windowattention_b_kernel(
 
         for cb in range(CB):
             nc.sync.dma_start(x_sb[0][:, cb, :], x_blocks[:, cb, 0:CHUNK])
-            nc.sync.dma_start(w_k[:, cb, :], qkv_blocks[:, cb, C : 2 * C])
+            nc.scalar.dma_start(w_k[:, cb, :], qkv_blocks[:, cb, C : 2 * C])
             if cb == 0:
                 with nc.allow_non_contiguous_dma(reason="512 biases, one to a partition and column"):
                     nc.sync.dma_start(proj_b_sb[:], proj_b.rearrange("(k p) one -> p (k one)", p=P))
@@ -215,7 +215,7 @@ def tile_windowattention_b_kernel(
             if not 0 <= b < NW:
                 return
             if h == 0:
-                a_ps[b] = attended.tile([P, H, T], F32, name="a_ps")
+                a_ps[b] = attended.tile([P, H, T], BF16, name="a_ps")
             nc.tensor.matmul(
                 a_ps[b][:, h, :], v_sb[b][:, h * HD : (h + 1) * HD], pT_sb[b][:, h, :], start=True, stop=True
             )
@@ -261,12 +261,12 @@ def tile_windowattention_b_kernel(
             q_out(t + 1, w)
             exponentials(i)
         last = NW - 1
-        for h in range(H):
-            flip_matmul(last, h)
-        flip_out(last)
         for cb in range(CB):
             v_matmul(last, cb)
         v_out(last)
+        for h in range(H):
+            flip_matmul(last, h)
+        flip_out(last)
         for h in range(H):
             attend_matmul(last - 1, h)
         attend_out(last - 1)

@@ -21,9 +21,10 @@ LAG = 4
 FLOPS = 2 * C * 3 * C * N + 2 * 2 * NW * H * T * T * HD + 2 * C * C * N
 
 BF16, F32, U16 = mybir.dt.bfloat16, mybir.dt.float32, mybir.dt.uint16
-ADD, MULT, MAX = mybir.AluOpType.add, mybir.AluOpType.mult, mybir.AluOpType.max
+ADD, MAX = mybir.AluOpType.add, mybir.AluOpType.max
 EXP = mybir.ActivationFunctionType.Exp
 IDENTITY = mybir.ActivationFunctionType.Identity
+COPY = mybir.ActivationFunctionType.Copy
 
 
 def tile_windowattention_b_kernel(
@@ -196,7 +197,8 @@ def tile_windowattention_b_kernel(
             r_sum = stats.tile([P, H], F32, name="r_sum")
             nc.vector.reciprocal(r_sum[:], e_sum[b][:])
             p_sb[b] = probs.tile([P, H, T], BF16, name="p_sb")
-            nc.gpsimd.tensor_tensor(p_sb[b][:], e_sb[b][:], r_sum[:].unsqueeze(2).to_broadcast([P, H, T]), MULT)
+            for h in range(H):
+                nc.scalar.activation(p_sb[b][:, h, :], e_sb[b][:, h, :], COPY, scale=r_sum[:, h : h + 1])
 
         def flip_matmul(b, h):
             if not 0 <= b < NW:

@@ -61,12 +61,10 @@ def tile_windowattention_b_kernel(
         for cb in range(CB):
             nc.sync.dma_start(x_sb[0][:, cb, :], x_blocks[:, cb, 0:CHUNK])
             nc.scalar.dma_start(w_k[:, cb, :], qkv_blocks[:, cb, C : 2 * C])
-            if cb == 0:
-                with nc.allow_non_contiguous_dma(reason="512 biases, one to a partition and column"):
-                    nc.sync.dma_start(proj_b_sb[:], proj_b.rearrange("(k p) one -> p (k one)", p=P))
         nc.sync.dma_start(w_q[:], qkv_blocks[:, :, 0:C])
         with nc.allow_non_contiguous_dma(reason="512 biases, one to a partition and column"):
             nc.sync.dma_start(q_b_sb[:], q_b.rearrange("(k p) one -> p (k one)", p=P))
+            nc.sync.dma_start(proj_b_sb[:], proj_b.rearrange("(k p) one -> p (k one)", p=P))
         nc.sync.dma_start(rel_sb[:], rel_bias.rearrange("h n m -> n h m"))
         nc.sync.dma_start(mask_sb[:], mask.rearrange("i n m -> n i m"))
         nc.sync.dma_start(x_sb[1][:], x_blocks[:, :, CHUNK : 2 * CHUNK])
@@ -90,8 +88,6 @@ def tile_windowattention_b_kernel(
             )
 
         proj_b_rows = [held.tile([P, N], F32, name=f"proj_b_rows{ob}") for ob in range(CB)]
-        for ob in range(CB):
-            nc.vector.tensor_copy(proj_b_rows[ob][:], proj_b_sb[:, ob : ob + 1].to_broadcast([P, N]))
 
         k_ps, q_ps, v_ps, y_ps, s_ps, pT_ps, a_ps = {}, {}, {}, {}, {}, {}, {}
         k_sb, q_sb = {}, {}
@@ -262,6 +258,8 @@ def tile_windowattention_b_kernel(
             attend_out(done)
             q_out(t + 1, w)
             exponentials(i)
+            if i < CB:
+                nc.vector.tensor_copy(proj_b_rows[i][:], proj_b_sb[:, i : i + 1].to_broadcast([P, N]))
         last = NW - 1
         for cb in range(CB):
             v_matmul(last, cb)

import math

import concourse.mybir as mybir
from concourse.masks import make_identity

P = 128
C = 512
N = 2048
S = 4096
H = 4
HD = 128
T = 128
NM = 4
CB = C // P
NW = N // T
CHUNK = 512
NCH = N // CHUNK
WPC = CHUNK // T
LAG = 4

FLOPS = 2 * C * 3 * C * N + 2 * 2 * NW * H * T * T * HD + 2 * C * C * N

BF16, F32, U16 = mybir.dt.bfloat16, mybir.dt.float32, mybir.dt.uint16
ADD, MAX = mybir.AluOpType.add, mybir.AluOpType.max
EXP = mybir.ActivationFunctionType.Exp
IDENTITY = mybir.ActivationFunctionType.Identity
COPY = mybir.ActivationFunctionType.Copy


def tile_windowattention_b_kernel(
    tc, x, qkv_w, q_b, v_b, rel_bias, mask, proj_w, proj_b, base, offs, out
):
    nc = tc.nc
    inv_sqrt_hd = 1.0 / math.sqrt(HD)
    with (
        tc.tile_pool(name="held", bufs=1) as held,
        tc.tile_pool(name="chunked", bufs=2) as chunked,
        tc.tile_pool(name="ring", bufs=3) as ring,
        tc.tile_pool(name="probs", bufs=LAG + 2) as probs,
        tc.tile_pool(name="stats", bufs=4) as stats,
        tc.psum_pool(name="acc", bufs=4) as acc,
        tc.psum_pool(name="scored", bufs=2) as scored,
        tc.psum_pool(name="flipped", bufs=1) as flipped,
        tc.psum_pool(name="attended", bufs=1) as attended,
    ):
        x_blocks = x.rearrange("(cb p) n -> p cb n", p=P)
        qkv_blocks = qkv_w.rearrange("(cb p) o -> p cb o", p=P)
        offsets = held.tile([P, N // 16], U16, name="offsets")
        x_sb = [held.tile([P, CB, CHUNK], BF16, name=f"x{t}") for t in range(NCH)]
        w_q = held.tile([P, CB, C], BF16, name="w_q")
        w_k = held.tile([P, CB, C], BF16, name="w_k")
        w_v = held.tile([P, CB, C], BF16, name="w_v")
        w_p = held.tile([P, CB, C], BF16, name="w_p")
        q_b_sb = held.tile([P, CB], F32, name="q_b_sb")
        proj_b_sb = held.tile([P, CB], F32, name="proj_b_sb")
        rel_sb = held.tile([P, H, T], F32, name="rel_sb")
        mask_sb = held.tile([P, NM, T], F32, name="mask_sb")
        v_b_rows = held.tile([P, C], F32, name="v_b_rows")
        window = [held.tile([P, S], F32, name=f"window{ob}") for ob in range(CB)]

        for cb in range(CB):
            nc.sync.dma_start(x_sb[0][:, cb, :], x_blocks[:, cb, 0:CHUNK])
            nc.scalar.dma_start(w_k[:, cb, :], qkv_blocks[:, cb, C : 2 * C])
        nc.sync.dma_start(w_q[:], qkv_blocks[:, :, 0:C])
        with nc.allow_non_contiguous_dma(reason="512 biases, one to a partition and column"):
            nc.sync.dma_start(q_b_sb[:], q_b.rearrange("(k p) one -> p (k one)", p=P))
            nc.sync.dma_start(proj_b_sb[:], proj_b.rearrange("(k p) one -> p (k one)", p=P))
        nc.sync.dma_start(rel_sb[:], rel_bias.rearrange("h n m -> n h m"))
        nc.sync.dma_start(mask_sb[:], mask.rearrange("i n m -> n i m"))
        nc.sync.dma_start(x_sb[1][:], x_blocks[:, :, CHUNK : 2 * CHUNK])
        nc.sync.dma_start(w_v[:], qkv_blocks[:, :, 2 * C : 3 * C])
        nc.sync.dma_start(v_b_rows[:], v_b.rearrange("c one -> (c one)").partition_broadcast(P))
        for t in range(2, NCH):
            nc.sync.dma_start(x_sb[t][:], x_blocks[:, :, t * CHUNK : (t + 1) * CHUNK])
        nc.sync.dma_start(w_p[:], proj_w.rearrange("(cb p) o -> p cb o", p=P))
        nc.sync.dma_start(offsets[:], offs)
        for ob in range(CB):
            nc.sync.dma_start(window[ob][:], base[ob * P : (ob + 1) * P, :])

        ident = held.tile([P, P], BF16, name="ident")
        make_identity(nc, ident[:])
        q_b_scaled = held.tile([P, CB], F32, name="q_b_scaled")
        nc.gpsimd.tensor_scalar_mul(q_b_scaled[:], q_b_sb[:], inv_sqrt_hd)
        score_bias = [held.tile([P, H, T], F32, name=f"score_bias{i}") for i in range(NM)]
        for i in range(NM):
            nc.gpsimd.tensor_tensor(
                score_bias[i][:], rel_sb[:], mask_sb[:, i, :].unsqueeze(1).to_broadcast([P, H, T]), ADD
            )

        proj_b_rows = [held.tile([P, N], F32, name=f"proj_b_rows{ob}") for ob in range(CB)]

        k_ps, q_ps, v_ps, y_ps, s_ps, pT_ps, a_ps = {}, {}, {}, {}, {}, {}, {}
        k_sb, q_sb = {}, {}
        v_sb = {}
        s_sb, neg_max, e_sb, e_sum = {}, {}, {}, {}
        p_sb, pT_sb = {}, {}
        a_sb = [held.tile([P, H, CHUNK], BF16, name=f"a{t}") for t in range(NCH)]
        y_sb = [held.tile([P, N], F32, name=f"y{ob}") for ob in range(CB)]

        def k_matmul(t, h, cb):
            if t >= NCH:
                return
            if cb == 0:
                k_ps[t, h] = acc.tile([P, CHUNK], F32, name="acc_ps")
            nc.tensor.matmul(
                k_ps[t, h][:], w_k[:, cb, h * HD : (h + 1) * HD], x_sb[t][:, cb, :], start=(cb == 0), stop=(cb == CB - 1)
            )

        def k_out(t, h):
            if t >= NCH:
                return
            if h == 0:
                k_sb[t] = chunked.tile([P, H, CHUNK], BF16, name="k_sb")
            nc.vector.tensor_copy(k_sb[t][:, h, :], k_ps[t, h][:])

        def q_matmul(t, h, cb):
            if t >= NCH:
                return
            if cb == 0:
                q_ps[t, h] = acc.tile([P, CHUNK], F32, name="acc_ps")
            nc.tensor.matmul(
                q_ps[t, h][:], w_q[:, cb, h * HD : (h + 1) * HD], x_sb[t][:, cb, :], start=(cb == 0), stop=(cb == CB - 1)
            )

        def q_out(t, h):
            if t >= NCH:
                return
            if h == 0:
                q_sb[t] = chunked.tile([P, H, CHUNK], BF16, name="q_sb")
            nc.scalar.activation(
                q_sb[t][:, h, :], q_ps[t, h][:], IDENTITY, bias=q_b_scaled[:, h : h + 1], scale=inv_sqrt_hd
            )

        def v_matmul(b, cb):
            if not 0 <= b < NW:
                return
            t, w = divmod(b, WPC)
            if cb == 0:
                v_ps[b] = acc.tile([P, C], F32, name="acc_ps")
            nc.tensor.matmul(
                v_ps[b][:], x_sb[t][:, cb, w * T : (w + 1) * T], w_v[:, cb, :], start=(cb == 0), stop=(cb == CB - 1)
            )

        def v_out(b):
            if not 0 <= b < NW:
                return
            v_sb[b] = ring.tile([P, C], BF16, name="v_sb")
            nc.vector.tensor_tensor(v_sb[b][:], v_ps[b][:], v_b_rows[:], ADD)

        def y_matmul(ob, t, h, w0=0, w1=WPC):
            if h == 0:
                y_ps[ob, t, w0] = acc.tile([P, CHUNK], F32, name="acc_ps")
            tokens = slice(w0 * T, w1 * T)
            nc.tensor.matmul(
                y_ps[ob, t, w0][:, tokens], w_p[:, h, ob * P : (ob + 1) * P], a_sb[t][:, h, tokens],
                start=(h == 0), stop=(h == H - 1),
            )

        def y_out(ob, t, w0=0, w1=WPC, copy=nc.scalar.copy):
            copy(y_sb[ob][:, t * CHUNK + w0 * T : t * CHUNK + w1 * T], y_ps[ob, t, w0][:, w0 * T : w1 * T])

        def score_matmul(b, h):
            if not 0 <= b < NW:
                return
            t, w = divmod(b, WPC)
            tokens = slice(w * T, (w + 1) * T)
            if h == 0:
                s_ps[b] = scored.tile([P, H, T], F32, name="s_ps")
            nc.tensor.matmul(s_ps[b][:, h, :], q_sb[t][:, h, tokens], k_sb[t][:, h, tokens], start=True, stop=True)

        def score_out(b):
            if not 0 <= b < NW:
                return
            s_sb[b] = ring.tile([P, H, T], F32, name="s_sb")
            nc.vector.tensor_tensor(s_sb[b][:], s_ps[b][:], score_bias[b % NM][:], ADD)
            neg_max[b] = stats.tile([P, H], F32, name="neg_max")
            nc.vector.tensor_reduce(neg_max[b][:], s_sb[b][:], axis=mybir.AxisListType.X, op=MAX, negate=True)

        def exponentials(b):
            if not 0 <= b < NW:
                return
            e_sb[b] = ring.tile([P, H, T], F32, name="e_sb")
            e_sum[b] = stats.tile([P, H], F32, name="e_sum")
            for h in range(H):
                nc.scalar.activation(
                    e_sb[b][:, h, :], s_sb[b][:, h, :], EXP, bias=neg_max[b][:, h : h + 1], scale=1.0,
                    accum_out=e_sum[b][:, h : h + 1],
                )

        def normalise(b):
            if not 0 <= b < NW:
                return
            r_sum = stats.tile([P, H], F32, name="r_sum")
            nc.vector.reciprocal(r_sum[:], e_sum[b][:])
            p_sb[b] = probs.tile([P, H, T], BF16, name="p_sb")
            for h in range(H):
                nc.scalar.activation(p_sb[b][:, h, :], e_sb[b][:, h, :], COPY, scale=r_sum[:, h : h + 1])

        def flip_matmul(b, h):
            if not 0 <= b < NW:
                return
            if h == 0:
                pT_ps[b] = flipped.tile([P, H, T], BF16, name="pT_ps")
            nc.tensor.transpose(pT_ps[b][:, h, :], p_sb[b][:, h, :], ident[:])

        def flip_out(b):
            if not 0 <= b < NW:
                return
            pT_sb[b] = ring.tile([P, H, T], BF16, name="pT_sb")
            nc.vector.tensor_copy(pT_sb[b][:], pT_ps[b][:])

        def attend_matmul(b, h):
            if not 0 <= b < NW:
                return
            if h == 0:
                a_ps[b] = attended.tile([P, H, T], BF16, name="a_ps")
            nc.tensor.matmul(
                a_ps[b][:, h, :], v_sb[b][:, h * HD : (h + 1) * HD], pT_sb[b][:, h, :], start=True, stop=True
            )

        def attend_out(b):
            if not 0 <= b < NW:
                return
            t, w = divmod(b, WPC)
            nc.scalar.copy(a_sb[t][:, :, w * T : (w + 1) * T], a_ps[b][:])

        for h in range(H):
            for cb in range(CB):
                k_matmul(0, h, cb)
            k_out(0, h)
        for h in range(H):
            for cb in range(CB):
                q_matmul(0, h, cb)
            q_out(0, h)
        for i in range(NW + LAG - 2):
            t, w = divmod(i, WPC)
            done = i - LAG
            normalise(done + 2)
            for j in range(4):
                v_matmul(done + 1, j)
                flip_matmul(done + 1, j)
            flip_out(done + 1)
            v_out(done + 1)
            spare = (i - (NW - WPC)) // 2
            fill_y = NW - WPC <= i < NW and w % 2 == 0
            for j in range(4):
                k_matmul(t + 1, w, j)
                if fill_y:
                    y_matmul(0, spare, j)
                score_matmul(i, j)
            k_out(t + 1, w)
            if fill_y:
                y_out(0, spare)
            score_out(i)
            for j in range(4):
                q_matmul(t + 1, w, j)
                attend_matmul(done, j)
            attend_out(done)
            q_out(t + 1, w)
            exponentials(i)
            if i < CB:
                nc.vector.tensor_copy(proj_b_rows[i][:], proj_b_sb[:, i : i + 1].to_broadcast([P, N]))
        last = NW - 1
        for cb in range(CB):
            v_matmul(last, cb)
        v_out(last)
        for h in range(H):
            flip_matmul(last, h)
        flip_out(last)
        for h in range(H):
            attend_matmul(last - 1, h)
        attend_out(last - 1)
        for h in range(H):
            y_matmul(0, NCH - 2, h)
        y_out(0, NCH - 2)
        for h in range(H):
            attend_matmul(last, h)
        attend_out(last)
        for h in range(H):
            y_matmul(0, NCH - 1, h, 0, WPC - 1)
        y_out(0, NCH - 1, 0, WPC - 1, copy=nc.vector.tensor_copy)
        for h in range(H):
            y_matmul(0, NCH - 1, h, WPC - 1, WPC)
        y_out(0, NCH - 1, WPC - 1, WPC)

        for ob in range(CB):
            if ob > 0:
                for t in range(NCH):
                    for h in range(H):
                        y_matmul(ob, t, h)
                    y_out(ob, t)
            nc.vector.tensor_tensor(window[ob][:].indirect(offsets[:]), y_sb[ob][:], proj_b_rows[ob][:], ADD)
            nc.sync.dma_start(out[ob * P : (ob + 1) * P, :], window[ob][:])
